import numpy as np
import ml_dtypes


def mxq(x, axis, fmt="e4m3"):
    dtype, down = {"e4m3": (ml_dtypes.float8_e4m3fn, 7), "e5m2": (ml_dtypes.float8_e5m2, 14)}[fmt]
    v = np.moveaxis(np.asarray(x, np.float32).astype(ml_dtypes.bfloat16).astype(np.float64), axis, -1)
    blocks = v.reshape(v.shape[:-1] + (-1, 32))
    amax = np.abs(blocks).max(-1, keepdims=True)
    byte = np.maximum(np.where(amax > 0, np.frexp(amax)[1] - 1 + 127, 0) - down, 1)
    scale = np.exp2(byte - 127.0)
    codes = (blocks / scale).astype(np.float32).astype(dtype).astype(np.float64)
    return np.moveaxis((codes * scale).reshape(v.shape), -1, axis)


WIDE = False


def mx_kscale(k):
    if not WIDE:
        return np.ones(k)
    levels = np.array([10, -10, 5, -5, 0])
    a = np.random.permutation(np.resize(levels, k // 512 * 4)).reshape(k // 512, 4)
    idx = np.arange(k)
    return np.exp2(a[idx // 512, idx % 128 // 32])


BF16 = ml_dtypes.bfloat16


def bf(x):
    return np.asarray(x, np.float32).astype(BF16)


def f64(x):
    return np.asarray(x).astype(np.float64)


B, S, D = 4, 1024, 512


def setup_inputs():
    s = mx_kscale(D)
    return {"X": bf(np.random.standard_normal((B, S, D)) * s),
            "Wq": bf(np.random.standard_normal((D, D)) * 2.5 / np.sqrt(D) / s[:, None]),
            "bq": bf(np.random.standard_normal(D) * 0.3),
            "Wv": bf(np.random.standard_normal((D, D)) / np.sqrt(D) / s[:, None]),
            "bv": bf(np.random.standard_normal(D) * 0.3)}


def reference(X, Wq, bq, Wv, bv):
    xq = mxq(f64(X), 2, "e4m3")
    q = (xq @ mxq(f64(Wq), 0, "e4m3")) + f64(bq)
    v = (xq @ mxq(f64(Wv), 0, "e4m3")) + f64(bv)
    v_viewed = np.reshape(v, (B, D, S))
    scores = (mxq(q, 2, "e4m3") @ mxq(v_viewed, 1, "e4m3")) / np.sqrt(D)
    return scores, v

@@ -1,0 +1,227 @@
+import math
+from contextlib import ExitStack
+
+import concourse.mybir as mybir
+from concourse.masks import make_identity
+
+BF16 = mybir.dt.bfloat16
+F32 = mybir.dt.float32
+U32 = mybir.dt.uint32
+U8 = mybir.dt.uint8
+FP8X4 = mybir.dt.float8_e4m3fn_x4
+ADD = mybir.AluOpType.add
+MULT = mybir.AluOpType.mult
+
+B, S, D = 4, 1024, 512
+P = 128
+PACK = 4
+TOKEN_TILES = S // P
+HALVES = 2
+QUANT_TILES = 4
+STORE_TILES = 2
+INV_SQRT_D = 1.0 / math.sqrt(D)
+
+FLOPS = 2 * B * S * D * D * 2 + 2 * B * S * D * S
+
+
+def tile_selfattention_pa_t_kernel(tc, X, Wq, bq, Wv, bv, out_0, out_1):
+    nc = tc.nc
+    with ExitStack() as stack:
+        stack.enter_context(tc.manual_schedule())
+        const = stack.enter_context(tc.tile_pool(name="const", bufs=1))
+        x_pool = stack.enter_context(tc.tile_pool(name="x_in", bufs=B))
+        work = stack.enter_context(tc.tile_pool(name="work", bufs=2))
+        score_pool = stack.enter_context(tc.tile_pool(name="score_out", bufs=5))
+        psum = stack.enter_context(tc.psum_pool(name="psum", bufs=4))
+
+        def tile_cols(m, count=1):
+            return slice(m * P, (m + count) * P)
+
+        def half_cols(h):
+            return slice(h * D, (h + 1) * D)
+
+        def load_x(b):
+            x_sb = x_pool.tile([P, TOKEN_TILES, D], BF16, tag="x")
+            x_rows = X[b].rearrange("(p m) d -> p m d", m=TOKEN_TILES)
+            for m0 in range(0, TOKEN_TILES, QUANT_TILES):
+                tiles = slice(m0, m0 + QUANT_TILES)
+                nc.sync.dma_start(out=x_sb[:, tiles, :], in_=x_rows[:, tiles, :])
+            return x_sb
+
+        def load_weight(w, name):
+            raw = const.tile([P, PACK, D], BF16, name=name)
+            nc.sync.dma_start(
+                out=raw[:].rearrange("p (u e) c -> p u e c", u=2),
+                in_=w.rearrange("(u p e) c -> p u e c", u=2, e=2),
+            )
+            return raw
+
+        def quantise(grouped, codes, scales):
+            nc.vector.quantize_mx(out=codes.bitcast(FP8X4), scales=scales, in_=grouped)
+
+        def quantise_tiles(grouped, mx, m0):
+            quantise(
+                grouped[:, m0 : m0 + QUANT_TILES].rearrange("p m k t -> p (m k t)"),
+                mx[0][:, tile_cols(m0, QUANT_TILES)],
+                mx[1][:, tile_cols(m0, QUANT_TILES)],
+            )
+
+        def new_mx(name):
+            codes = work.tile([P, S], U32, align_bytes=64, name=name + "_codes")
+            scales = work.tile([P, S], U8, align_bytes=64, name=name + "_scales")
+            return codes, scales
+
+        def mx_pass(acc, lhs, lhs_cols, rhs, rhs_cols):
+            nc.tensor.matmul_mx(
+                out=acc,
+                lhsT=lhs[0][:, lhs_cols].bitcast(FP8X4),
+                lhsT_scale=lhs[1][:, lhs_cols],
+                rhs=rhs[0][:, rhs_cols].bitcast(FP8X4),
+                rhs_scale=rhs[1][:, rhs_cols],
+                start=True,
+                stop=True,
+            )
+
+        wv_raw = load_weight(Wv, "wv_raw")
+        wq_raw = load_weight(Wq, "wq_raw")
+        x_tiles = [load_x(b) for b in range(B)]
+        bq_sb = const.tile([P, PACK], BF16)
+        nc.scalar.dma_start(out=bq_sb[:], in_=bq.rearrange("(p t) -> p t", t=PACK))
+        bv_bc = const.tile([P, D], BF16)
+        nc.scalar.dma_start(out=bv_bc[:], in_=bv.partition_broadcast(P))
+
+        ident = const.tile([P, P], F32)
+        make_identity(nc, ident[:])
+
+        wv_grouped = const.tile([P, D, PACK], BF16, align_bytes=64)
+        nc.vector.tensor_copy(out=wv_grouped[:], in_=wv_raw[:].rearrange("p t c -> p c t"))
+        wq_grouped = const.tile([P, PACK, P, PACK], BF16, align_bytes=64)
+        nc.vector.tensor_copy(
+            out=wq_grouped[:], in_=wq_raw[:].rearrange("p t (j i) -> p i j t", i=PACK)
+        )
+        wv_codes = const.tile([P, D], U32, align_bytes=64)
+        wv_scales = const.tile([P, D], U8, align_bytes=64)
+        quantise(wv_grouped[:].rearrange("p c t -> p (c t)"), wv_codes[:], wv_scales[:])
+        wq_codes = const.tile([P, D], U32, align_bytes=64)
+        wq_scales = const.tile([P, D], U8, align_bytes=64)
+        quantise(wq_grouped[:].rearrange("p i j t -> p (i j t)"), wq_codes[:], wq_scales[:])
+        wv_mx = (wv_codes, wv_scales)
+        wq_mx = (wq_codes, wq_scales)
+
+        def transpose_x(b):
+            x_words = x_tiles[b][:].bitcast(F32)
+            x_grouped = work.tile([P, TOKEN_TILES, P, PACK], BF16, align_bytes=64)
+            x_grouped_words = x_grouped[:].bitcast(F32)
+            banks = []
+            for m0 in range(0, TOKEN_TILES, 2):
+                xt = psum.tile([P, 2, 2, P], F32, tag="side")
+                for i in range(2):
+                    for u in range(2):
+                        nc.tensor.transpose(
+                            xt[:, i, u, :], x_words[:, m0 + i, u * P : (u + 1) * P], ident[:]
+                        )
+                banks.append(xt)
+            for n in range(len(banks)):
+                nc.scalar.copy(
+                    out=x_grouped_words[:, 2 * n : 2 * n + 2, :, :],
+                    in_=banks[n][:].rearrange("p i u k -> p i k u"),
+                )
+            return x_grouped
+
+        def value_bank(x_mx, v_sb, m):
+            acc = psum.tile([P, D], F32, tag="proj")
+            mx_pass(acc[:], x_mx, tile_cols(m), wv_mx, slice(0, D))
+            nc.vector.tensor_tensor(out=v_sb[:, m, :], in0=acc[:], in1=bv_bc[:], op=ADD)
+
+        def query_bank(x_mx, q_grouped, m):
+            acc = psum.tile([P, PACK, P], F32, tag="proj")
+            for t in range(PACK):
+                mx_pass(acc[:, t, :], wq_mx, tile_cols(t), x_mx, tile_cols(m))
+            nc.vector.tensor_tensor(
+                out=q_grouped[:, m],
+                in0=acc[:].rearrange("p t k -> p k t"),
+                in1=bq_sb[:].unsqueeze(1).to_broadcast([P, P, PACK]),
+                op=ADD,
+            )
+
+        def score_bank(q_mx, v_mx, m, h, out_cols, on_vector):
+            acc = psum.tile([P, D], F32, tag="side")
+            mx_pass(acc[:], q_mx, tile_cols(m), v_mx, half_cols(h))
+            if on_vector:
+                nc.vector.tensor_scalar_mul(out=out_cols, in0=acc[:], scalar1=INV_SQRT_D)
+            else:
+                nc.scalar.mul(out=out_cols, in_=acc[:], mul=INV_SQRT_D)
+
+        def store_scores(b, m0, score_sb):
+            score_rows = out_0[b].rearrange("(p m) j -> p m j", m=TOKEN_TILES)
+            nc.sync.dma_start(out=score_rows[:, m0 : m0 + STORE_TILES, :], in_=score_sb[:])
+
+        x_grouped = transpose_x(0)
+        x_mx = new_mx("x")
+        quantise_tiles(x_grouped, x_mx, 0)
+        quantise_tiles(x_grouped, x_mx, QUANT_TILES)
+        q_mx = None
+        v_mx = None
+
+        for b in range(B):
+            v_sb = work.tile([P, TOKEN_TILES, D], F32)
+            v_grouped = work.tile([P, HALVES, D, PACK], BF16, align_bytes=64)
+            v_by_half = v_sb[:].rearrange("p (t h) d -> p h d t", h=HALVES)
+            for h in range(HALVES):
+                m0 = QUANT_TILES + STORE_TILES * h
+                if b > 0:
+                    score_sb = score_pool.tile([P, STORE_TILES, HALVES * D], F32)
+                for t in range(PACK):
+                    value_bank(x_mx, v_sb, HALVES * t + h)
+                    if b > 0:
+                        i = t // HALVES
+                        g = t % HALVES
+                        score_bank(q_mx, v_mx, m0 + i, g, score_sb[:, i, half_cols(g)], False)
+                if h == 0:
+                    nc.gpsimd.tensor_scalar(
+                        out=v_grouped[:, h], in0=v_by_half[:, h],
+                        scalar1=1.0, scalar2=0.0, op0=MULT, op1=ADD,
+                    )
+                else:
+                    nc.scalar.copy(out=v_grouped[:, h], in_=v_by_half[:, h])
+                if b > 0:
+                    store_scores(b - 1, m0, score_sb)
+            nc.sync.dma_start(
+                out=out_1[b].rearrange("(p m) d -> p m d", m=TOKEN_TILES), in_=v_sb[:]
+            )
+
+            q_grouped = work.tile([P, TOKEN_TILES, P, PACK], BF16, align_bytes=64)
+            q_mx = new_mx("q")
+            v_mx = new_mx("v")
+            for m in range(QUANT_TILES):
+                query_bank(x_mx, q_grouped, m)
+            if b + 1 < B:
+                x_grouped = transpose_x(b + 1)
+            for h in range(HALVES):
+                quantise(
+                    v_grouped[:, h].rearrange("p d t -> p (d t)"),
+                    v_mx[0][:, half_cols(h)],
+                    v_mx[1][:, half_cols(h)],
+                )
+            quantise_tiles(q_grouped, q_mx, 0)
+            for m in range(QUANT_TILES, TOKEN_TILES):
+                query_bank(x_mx, q_grouped, m)
+            if b + 1 < B:
+                x_mx = new_mx("x")
+                quantise_tiles(x_grouped, x_mx, 0)
+                quantise_tiles(x_grouped, x_mx, QUANT_TILES)
+            quantise_tiles(q_grouped, q_mx, QUANT_TILES)
+
+            for m0 in range(0, QUANT_TILES, STORE_TILES):
+                score_sb = score_pool.tile([P, STORE_TILES, HALVES * D], F32)
+                for i in range(STORE_TILES):
+                    for g in range(HALVES):
+                        score_bank(q_mx, v_mx, m0 + i, g, score_sb[:, i, half_cols(g)], False)
+                store_scores(b, m0, score_sb)
+
+        for m0 in range(QUANT_TILES, TOKEN_TILES, STORE_TILES):
+            score_sb = score_pool.tile([P, STORE_TILES, HALVES * D], F32)
+            for i in range(STORE_TILES):
+                for g in range(HALVES):
+                    score_bank(q_mx, v_mx, m0 + i, g, score_sb[:, i, half_cols(g)], g == 1)
+            store_scores(B - 1, m0, score_sb)

@@ -66,6 +66,13 @@ def tile_selfattention_pa_t_kernel(tc, X, Wq, bq, Wv, bv, out_0, out_1):
                 mx[1][:, tile_cols(m0, QUANT_TILES)],
             )
 
+        def quantise_half(v_grouped, mx, h):
+            quantise(
+                v_grouped[:, h].rearrange("p d t -> p (d t)"),
+                mx[0][:, half_cols(h)],
+                mx[1][:, half_cols(h)],
+            )
+
         def new_mx(name):
             codes = work.tile([P, S], U32, align_bytes=64, name=name + "_codes")
             scales = work.tile([P, S], U8, align_bytes=64, name=name + "_scales")
@@ -82,13 +89,21 @@ def tile_selfattention_pa_t_kernel(tc, X, Wq, bq, Wv, bv, out_0, out_1):
                 stop=True,
             )
 
+        bv_row = const.tile([P, D], BF16)
+        nc.vector.memset(bv_row[:], 0.0)
+        nc.sync.dma_start(out=bv_row[0:1, :], in_=bv.rearrange("(o d) -> o d", o=1))
+        bq_sb = const.tile([P, PACK], BF16)
+        nc.sync.dma_start(out=bq_sb[:], in_=bq.rearrange("(p t) -> p t", t=PACK))
         wv_raw = load_weight(Wv, "wv_raw")
         wq_raw = load_weight(Wq, "wq_raw")
         x_tiles = [load_x(b) for b in range(B)]
-        bq_sb = const.tile([P, PACK], BF16)
-        nc.scalar.dma_start(out=bq_sb[:], in_=bq.rearrange("(p t) -> p t", t=PACK))
-        bv_bc = const.tile([P, D], BF16)
-        nc.scalar.dma_start(out=bv_bc[:], in_=bv.partition_broadcast(P))
+
+        ones = const.tile([P, P], BF16)
+        nc.vector.memset(ones[:], 1.0)
+        bv_acc = psum.tile([P, D], F32, tag="side")
+        nc.tensor.matmul(out=bv_acc[:], lhsT=ones[:], rhs=bv_row[:], start=True, stop=True)
+        bv_bc = const.tile([P, D], F32)
+        nc.scalar.copy(out=bv_bc[:], in_=bv_acc[:])
 
         ident = const.tile([P, P], F32)
         make_identity(nc, ident[:])
@@ -152,7 +167,13 @@ def tile_selfattention_pa_t_kernel(tc, X, Wq, bq, Wv, bv, out_0, out_1):
             else:
                 nc.scalar.mul(out=out_cols, in_=acc[:], mul=INV_SQRT_D)
 
-        def store_scores(b, m0, score_sb):
+        def score_pair(b, q_mx, v_mx, m0, vector_helps):
+            score_sb = score_pool.tile([P, STORE_TILES, HALVES * D], F32)
+            for i in range(STORE_TILES):
+                for h in range(HALVES):
+                    score_bank(
+                        q_mx, v_mx, m0 + i, h, score_sb[:, i, half_cols(h)], vector_helps and h == 1
+                    )
             score_rows = out_0[b].rearrange("(p m) j -> p m j", m=TOKEN_TILES)
             nc.sync.dma_start(out=score_rows[:, m0 : m0 + STORE_TILES, :], in_=score_sb[:])
 
@@ -168,24 +189,16 @@ def tile_selfattention_pa_t_kernel(tc, X, Wq, bq, Wv, bv, out_0, out_1):
             v_grouped = work.tile([P, HALVES, D, PACK], BF16, align_bytes=64)
             v_by_half = v_sb[:].rearrange("p (t h) d -> p h d t", h=HALVES)
             for h in range(HALVES):
-                m0 = QUANT_TILES + STORE_TILES * h
-                if b > 0:
-                    score_sb = score_pool.tile([P, STORE_TILES, HALVES * D], F32)
                 for t in range(PACK):
                     value_bank(x_mx, v_sb, HALVES * t + h)
-                    if b > 0:
-                        i = t // HALVES
-                        g = t % HALVES
-                        score_bank(q_mx, v_mx, m0 + i, g, score_sb[:, i, half_cols(g)], False)
-                if h == 0:
-                    nc.gpsimd.tensor_scalar(
-                        out=v_grouped[:, h], in0=v_by_half[:, h],
-                        scalar1=1.0, scalar2=0.0, op0=MULT, op1=ADD,
-                    )
-                else:
-                    nc.scalar.copy(out=v_grouped[:, h], in_=v_by_half[:, h])
                 if b > 0:
-                    store_scores(b - 1, m0, score_sb)
+                    score_pair(b - 1, q_mx, v_mx, QUANT_TILES + STORE_TILES * h, False)
+                gpsimd_cols = slice(0, D) if h == 0 else slice(0, D // 2)
+                nc.gpsimd.tensor_scalar(
+                    out=v_grouped[:, h, gpsimd_cols], in0=v_by_half[:, h, gpsimd_cols],
+                    scalar1=1.0, scalar2=0.0, op0=MULT, op1=ADD,
+                )
+            nc.scalar.copy(out=v_grouped[:, 1, D // 2 : D], in_=v_by_half[:, 1, D // 2 : D])
             nc.sync.dma_start(
                 out=out_1[b].rearrange("(p m) d -> p m d", m=TOKEN_TILES), in_=v_sb[:]
             )
@@ -197,13 +210,9 @@ def tile_selfattention_pa_t_kernel(tc, X, Wq, bq, Wv, bv, out_0, out_1):
                 query_bank(x_mx, q_grouped, m)
             if b + 1 < B:
                 x_grouped = transpose_x(b + 1)
-            for h in range(HALVES):
-                quantise(
-                    v_grouped[:, h].rearrange("p d t -> p (d t)"),
-                    v_mx[0][:, half_cols(h)],
-                    v_mx[1][:, half_cols(h)],
-                )
+            quantise_half(v_grouped, v_mx, 0)
             quantise_tiles(q_grouped, q_mx, 0)
+            quantise_half(v_grouped, v_mx, 1)
             for m in range(QUANT_TILES, TOKEN_TILES):
                 query_bank(x_mx, q_grouped, m)
             if b + 1 < B:
@@ -212,16 +221,8 @@ def tile_selfattention_pa_t_kernel(tc, X, Wq, bq, Wv, bv, out_0, out_1):
                 quantise_tiles(x_grouped, x_mx, QUANT_TILES)
             quantise_tiles(q_grouped, q_mx, QUANT_TILES)
 
-            for m0 in range(0, QUANT_TILES, STORE_TILES):
-                score_sb = score_pool.tile([P, STORE_TILES, HALVES * D], F32)
-                for i in range(STORE_TILES):
-                    for g in range(HALVES):
-                        score_bank(q_mx, v_mx, m0 + i, g, score_sb[:, i, half_cols(g)], False)
-                store_scores(b, m0, score_sb)
+            score_pair(b, q_mx, v_mx, 0, False)
+            score_pair(b, q_mx, v_mx, STORE_TILES, b == B - 1)
 
         for m0 in range(QUANT_TILES, TOKEN_TILES, STORE_TILES):
-            score_sb = score_pool.tile([P, STORE_TILES, HALVES * D], F32)
-            for i in range(STORE_TILES):
-                for g in range(HALVES):
-                    score_bank(q_mx, v_mx, m0 + i, g, score_sb[:, i, half_cols(g)], g == 1)
-            store_scores(B - 1, m0, score_sb)
+            score_pair(B - 1, q_mx, v_mx, m0, True)

@@ -59,11 +59,11 @@ def tile_selfattention_pa_t_kernel(tc, X, Wq, bq, Wv, bv, out_0, out_1):
         def quantise(grouped, codes, scales):
             nc.vector.quantize_mx(out=codes.bitcast(FP8X4), scales=scales, in_=grouped)
 
-        def quantise_tiles(grouped, mx, m0):
+        def quantise_tiles(grouped, mx, m0, count):
             quantise(
-                grouped[:, m0 : m0 + QUANT_TILES].rearrange("p m k t -> p (m k t)"),
-                mx[0][:, tile_cols(m0, QUANT_TILES)],
-                mx[1][:, tile_cols(m0, QUANT_TILES)],
+                grouped[:, m0 : m0 + count].rearrange("p m k t -> p (m k t)"),
+                mx[0][:, tile_cols(m0, count)],
+                mx[1][:, tile_cols(m0, count)],
             )
 
         def quantise_half(v_grouped, mx, h):
@@ -91,10 +91,10 @@ def tile_selfattention_pa_t_kernel(tc, X, Wq, bq, Wv, bv, out_0, out_1):
 
         bv_row = const.tile([P, D], BF16)
         nc.vector.memset(bv_row[:], 0.0)
-        nc.sync.dma_start(out=bv_row[0:1, :], in_=bv.rearrange("(o d) -> o d", o=1))
         bq_sb = const.tile([P, PACK], BF16)
         nc.sync.dma_start(out=bq_sb[:], in_=bq.rearrange("(p t) -> p t", t=PACK))
         wv_raw = load_weight(Wv, "wv_raw")
+        nc.sync.dma_start(out=bv_row[0:1, :], in_=bv.rearrange("(o d) -> o d", o=1))
         wq_raw = load_weight(Wq, "wq_raw")
         x_tiles = [load_x(b) for b in range(B)]
 
@@ -169,8 +169,8 @@ def tile_selfattention_pa_t_kernel(tc, X, Wq, bq, Wv, bv, out_0, out_1):
 
         def score_pair(b, q_mx, v_mx, m0, vector_helps):
             score_sb = score_pool.tile([P, STORE_TILES, HALVES * D], F32)
-            for i in range(STORE_TILES):
-                for h in range(HALVES):
+            for h in range(HALVES):
+                for i in range(STORE_TILES):
                     score_bank(
                         q_mx, v_mx, m0 + i, h, score_sb[:, i, half_cols(h)], vector_helps and h == 1
                     )
@@ -179,8 +179,8 @@ def tile_selfattention_pa_t_kernel(tc, X, Wq, bq, Wv, bv, out_0, out_1):
 
         x_grouped = transpose_x(0)
         x_mx = new_mx("x")
-        quantise_tiles(x_grouped, x_mx, 0)
-        quantise_tiles(x_grouped, x_mx, QUANT_TILES)
+        quantise_tiles(x_grouped, x_mx, 0, QUANT_TILES)
+        quantise_tiles(x_grouped, x_mx, QUANT_TILES, QUANT_TILES)
         q_mx = None
         v_mx = None
 
@@ -206,20 +206,23 @@ def tile_selfattention_pa_t_kernel(tc, X, Wq, bq, Wv, bv, out_0, out_1):
             q_grouped = work.tile([P, TOKEN_TILES, P, PACK], BF16, align_bytes=64)
             q_mx = new_mx("q")
             v_mx = new_mx("v")
-            for m in range(QUANT_TILES):
+            for m in range(STORE_TILES):
                 query_bank(x_mx, q_grouped, m)
+            quantise_half(v_grouped, v_mx, 0)
+            quantise_tiles(q_grouped, q_mx, 0, STORE_TILES)
+            for m in range(STORE_TILES, QUANT_TILES):
+                query_bank(x_mx, q_grouped, m)
+            quantise_half(v_grouped, v_mx, 1)
+            quantise_tiles(q_grouped, q_mx, STORE_TILES, STORE_TILES)
             if b + 1 < B:
                 x_grouped = transpose_x(b + 1)
-            quantise_half(v_grouped, v_mx, 0)
-            quantise_tiles(q_grouped, q_mx, 0)
-            quantise_half(v_grouped, v_mx, 1)
             for m in range(QUANT_TILES, TOKEN_TILES):
                 query_bank(x_mx, q_grouped, m)
             if b + 1 < B:
                 x_mx = new_mx("x")
-                quantise_tiles(x_grouped, x_mx, 0)
-                quantise_tiles(x_grouped, x_mx, QUANT_TILES)
-            quantise_tiles(q_grouped, q_mx, QUANT_TILES)
+                quantise_tiles(x_grouped, x_mx, 0, QUANT_TILES)
+                quantise_tiles(x_grouped, x_mx, QUANT_TILES, QUANT_TILES)
+            quantise_tiles(q_grouped, q_mx, QUANT_TILES, QUANT_TILES)
 
             score_pair(b, q_mx, v_mx, 0, False)
             score_pair(b, q_mx, v_mx, STORE_TILES, b == B - 1)

@@ -59,11 +59,11 @@ def tile_selfattention_pa_t_kernel(tc, X, Wq, bq, Wv, bv, out_0, out_1):
         def quantise(grouped, codes, scales):
             nc.vector.quantize_mx(out=codes.bitcast(FP8X4), scales=scales, in_=grouped)
 
-        def quantise_tiles(grouped, mx, m0, count):
+        def quantise_tiles(grouped, mx, m0):
             quantise(
-                grouped[:, m0 : m0 + count].rearrange("p m k t -> p (m k t)"),
-                mx[0][:, tile_cols(m0, count)],
-                mx[1][:, tile_cols(m0, count)],
+                grouped[:, m0 : m0 + QUANT_TILES].rearrange("p m k t -> p (m k t)"),
+                mx[0][:, tile_cols(m0, QUANT_TILES)],
+                mx[1][:, tile_cols(m0, QUANT_TILES)],
             )
 
         def quantise_half(v_grouped, mx, h):
@@ -169,8 +169,8 @@ def tile_selfattention_pa_t_kernel(tc, X, Wq, bq, Wv, bv, out_0, out_1):
 
         def score_pair(b, q_mx, v_mx, m0, vector_helps):
             score_sb = score_pool.tile([P, STORE_TILES, HALVES * D], F32)
-            for h in range(HALVES):
-                for i in range(STORE_TILES):
+            for i in range(STORE_TILES):
+                for h in range(HALVES):
                     score_bank(
                         q_mx, v_mx, m0 + i, h, score_sb[:, i, half_cols(h)], vector_helps and h == 1
                     )
@@ -179,8 +179,8 @@ def tile_selfattention_pa_t_kernel(tc, X, Wq, bq, Wv, bv, out_0, out_1):
 
         x_grouped = transpose_x(0)
         x_mx = new_mx("x")
-        quantise_tiles(x_grouped, x_mx, 0, QUANT_TILES)
-        quantise_tiles(x_grouped, x_mx, QUANT_TILES, QUANT_TILES)
+        quantise_tiles(x_grouped, x_mx, 0)
+        quantise_tiles(x_grouped, x_mx, QUANT_TILES)
         q_mx = None
         v_mx = None
 
@@ -206,23 +206,20 @@ def tile_selfattention_pa_t_kernel(tc, X, Wq, bq, Wv, bv, out_0, out_1):
             q_grouped = work.tile([P, TOKEN_TILES, P, PACK], BF16, align_bytes=64)
             q_mx = new_mx("q")
             v_mx = new_mx("v")
-            for m in range(STORE_TILES):
+            for m in range(QUANT_TILES):
                 query_bank(x_mx, q_grouped, m)
-            quantise_half(v_grouped, v_mx, 0)
-            quantise_tiles(q_grouped, q_mx, 0, STORE_TILES)
-            for m in range(STORE_TILES, QUANT_TILES):
-                query_bank(x_mx, q_grouped, m)
-            quantise_half(v_grouped, v_mx, 1)
-            quantise_tiles(q_grouped, q_mx, STORE_TILES, STORE_TILES)
             if b + 1 < B:
                 x_grouped = transpose_x(b + 1)
+            quantise_half(v_grouped, v_mx, 0)
+            quantise_tiles(q_grouped, q_mx, 0)
+            quantise_half(v_grouped, v_mx, 1)
             for m in range(QUANT_TILES, TOKEN_TILES):
                 query_bank(x_mx, q_grouped, m)
             if b + 1 < B:
                 x_mx = new_mx("x")
-                quantise_tiles(x_grouped, x_mx, 0, QUANT_TILES)
-                quantise_tiles(x_grouped, x_mx, QUANT_TILES, QUANT_TILES)
-            quantise_tiles(q_grouped, q_mx, QUANT_TILES, QUANT_TILES)
+                quantise_tiles(x_grouped, x_mx, 0)
+                quantise_tiles(x_grouped, x_mx, QUANT_TILES)
+            quantise_tiles(q_grouped, q_mx, QUANT_TILES)
 
             score_pair(b, q_mx, v_mx, 0, False)
             score_pair(b, q_mx, v_mx, STORE_TILES, b == B - 1)

@@ -18,6 +18,7 @@ PACK = 4
 TOKEN_TILES = S // P
 HALVES = 2
 QUANT_TILES = 4
+PAIR = 2
 STORE_TILES = 2
 INV_SQRT_D = 1.0 / math.sqrt(D)
 
@@ -40,11 +41,11 @@ def tile_selfattention_pa_t_kernel(tc, X, Wq, bq, Wv, bv, out_0, out_1):
         def half_cols(h):
             return slice(h * D, (h + 1) * D)
 
-        def load_x(b):
+        def load_x(b, load_tiles):
             x_sb = x_pool.tile([P, TOKEN_TILES, D], BF16, tag="x")
             x_rows = X[b].rearrange("(p m) d -> p m d", m=TOKEN_TILES)
-            for m0 in range(0, TOKEN_TILES, QUANT_TILES):
-                tiles = slice(m0, m0 + QUANT_TILES)
+            for m0 in range(0, TOKEN_TILES, load_tiles):
+                tiles = slice(m0, m0 + load_tiles)
                 nc.sync.dma_start(out=x_sb[:, tiles, :], in_=x_rows[:, tiles, :])
             return x_sb
 
@@ -59,11 +60,11 @@ def tile_selfattention_pa_t_kernel(tc, X, Wq, bq, Wv, bv, out_0, out_1):
         def quantise(grouped, codes, scales):
             nc.vector.quantize_mx(out=codes.bitcast(FP8X4), scales=scales, in_=grouped)
 
-        def quantise_tiles(grouped, mx, m0):
+        def quantise_tiles(grouped, mx, m0, count):
             quantise(
-                grouped[:, m0 : m0 + QUANT_TILES].rearrange("p m k t -> p (m k t)"),
-                mx[0][:, tile_cols(m0, QUANT_TILES)],
-                mx[1][:, tile_cols(m0, QUANT_TILES)],
+                grouped[:, m0 : m0 + count].rearrange("p m k t -> p (m k t)"),
+                mx[0][:, tile_cols(m0, count)],
+                mx[1][:, tile_cols(m0, count)],
             )
 
         def quantise_half(v_grouped, mx, h):
@@ -92,55 +93,48 @@ def tile_selfattention_pa_t_kernel(tc, X, Wq, bq, Wv, bv, out_0, out_1):
         bv_row = const.tile([P, D], BF16)
         nc.vector.memset(bv_row[:], 0.0)
         bq_sb = const.tile([P, PACK], BF16)
-        nc.sync.dma_start(out=bq_sb[:], in_=bq.rearrange("(p t) -> p t", t=PACK))
         wv_raw = load_weight(Wv, "wv_raw")
+        x_tiles = [load_x(0, PAIR)]
         nc.sync.dma_start(out=bv_row[0:1, :], in_=bv.rearrange("(o d) -> o d", o=1))
         wq_raw = load_weight(Wq, "wq_raw")
-        x_tiles = [load_x(b) for b in range(B)]
+        nc.sync.dma_start(out=bq_sb[:], in_=bq.rearrange("(p t) -> p t", t=PACK))
+        x_tiles.extend(load_x(b, QUANT_TILES) for b in range(1, B))
 
         ones = const.tile([P, P], BF16)
         nc.vector.memset(ones[:], 1.0)
-        bv_acc = psum.tile([P, D], F32, tag="side")
-        nc.tensor.matmul(out=bv_acc[:], lhsT=ones[:], rhs=bv_row[:], start=True, stop=True)
-        bv_bc = const.tile([P, D], F32)
-        nc.scalar.copy(out=bv_bc[:], in_=bv_acc[:])
-
         ident = const.tile([P, P], F32)
         make_identity(nc, ident[:])
 
         wv_grouped = const.tile([P, D, PACK], BF16, align_bytes=64)
         nc.vector.tensor_copy(out=wv_grouped[:], in_=wv_raw[:].rearrange("p t c -> p c t"))
         wq_grouped = const.tile([P, PACK, P, PACK], BF16, align_bytes=64)
-        nc.vector.tensor_copy(
-            out=wq_grouped[:], in_=wq_raw[:].rearrange("p t (j i) -> p i j t", i=PACK)
-        )
         wv_codes = const.tile([P, D], U32, align_bytes=64)
         wv_scales = const.tile([P, D], U8, align_bytes=64)
-        quantise(wv_grouped[:].rearrange("p c t -> p (c t)"), wv_codes[:], wv_scales[:])
         wq_codes = const.tile([P, D], U32, align_bytes=64)
         wq_scales = const.tile([P, D], U8, align_bytes=64)
-        quantise(wq_grouped[:].rearrange("p i j t -> p (i j t)"), wq_codes[:], wq_scales[:])
         wv_mx = (wv_codes, wv_scales)
         wq_mx = (wq_codes, wq_scales)
 
-        def transpose_x(b):
+        def transpose_x(b, x_grouped, bank_list):
             x_words = x_tiles[b][:].bitcast(F32)
-            x_grouped = work.tile([P, TOKEN_TILES, P, PACK], BF16, align_bytes=64)
             x_grouped_words = x_grouped[:].bitcast(F32)
             banks = []
-            for m0 in range(0, TOKEN_TILES, 2):
+            for n in bank_list:
                 xt = psum.tile([P, 2, 2, P], F32, tag="side")
                 for i in range(2):
                     for u in range(2):
                         nc.tensor.transpose(
-                            xt[:, i, u, :], x_words[:, m0 + i, u * P : (u + 1) * P], ident[:]
+                            xt[:, i, u, :], x_words[:, 2 * n + i, u * P : (u + 1) * P], ident[:]
                         )
                 banks.append(xt)
-            for n in range(len(banks)):
+            for n, xt in zip(bank_list, banks):
                 nc.scalar.copy(
                     out=x_grouped_words[:, 2 * n : 2 * n + 2, :, :],
-                    in_=banks[n][:].rearrange("p i u k -> p i k u"),
+                    in_=xt[:].rearrange("p i u k -> p i k u"),
                 )
+
+        def new_grouped():
+            x_grouped = work.tile([P, TOKEN_TILES, P, PACK], BF16, align_bytes=64)
             return x_grouped
 
         def value_bank(x_mx, v_sb, m):
@@ -148,16 +142,39 @@ def tile_selfattention_pa_t_kernel(tc, X, Wq, bq, Wv, bv, out_0, out_1):
             mx_pass(acc[:], x_mx, tile_cols(m), wv_mx, slice(0, D))
             nc.vector.tensor_tensor(out=v_sb[:, m, :], in0=acc[:], in1=bv_bc[:], op=ADD)
 
-        def query_bank(x_mx, q_grouped, m):
+        def query_product(x_mx, m):
             acc = psum.tile([P, PACK, P], F32, tag="proj")
             for t in range(PACK):
                 mx_pass(acc[:, t, :], wq_mx, tile_cols(t), x_mx, tile_cols(m))
+            return acc
+
+        def query_bank(x_mx, q_grouped, m):
+            add_query_bias(query_product(x_mx, m), q_grouped, m)
+
+        def add_query_bias(acc, q_grouped, m):
             nc.vector.tensor_tensor(
                 out=q_grouped[:, m],
                 in0=acc[:].rearrange("p t k -> p k t"),
                 in1=bq_sb[:].unsqueeze(1).to_broadcast([P, P, PACK]),
                 op=ADD,
             )
+
+        def values(b, x_mx, v_sb, h):
+            for t in range(PACK):
+                value_bank(x_mx, v_sb, HALVES * t + h)
+            nc.sync.dma_start(
+                out=out_1[b].rearrange("(p t h) d -> p h t d", h=HALVES, t=PACK)[:, h],
+                in_=v_sb[:].rearrange("p (t h) d -> p h t d", h=HALVES)[:, h],
+            )
+
+        def regroup(v_sb, v_grouped, h, split):
+            v_by_half = v_sb[:].rearrange("p (t h) d -> p h d t", h=HALVES)
+            nc.gpsimd.tensor_scalar(
+                out=v_grouped[:, h, 0:split], in0=v_by_half[:, h, 0:split],
+                scalar1=1.0, scalar2=0.0, op0=MULT, op1=ADD,
+            )
+            if split < D:
+                nc.scalar.copy(out=v_grouped[:, h, split:D], in_=v_by_half[:, h, split:D])
 
         def score_bank(q_mx, v_mx, m, h, out_cols, on_vector):
             acc = psum.tile([P, D], F32, tag="side")
@@ -168,7 +185,7 @@ def tile_selfattention_pa_t_kernel(tc, X, Wq, bq, Wv, bv, out_0, out_1):
                 nc.scalar.mul(out=out_cols, in_=acc[:], mul=INV_SQRT_D)
 
         def score_pair(b, q_mx, v_mx, m0, vector_helps):
-            score_sb = score_pool.tile([P, STORE_TILES, HALVES * D], F32)
+            score_sb = score_pool.tile([P, STORE_TILES, HALVES * D], F32, tag="score_sb")
             for i in range(STORE_TILES):
                 for h in range(HALVES):
                     score_bank(
@@ -177,49 +194,95 @@ def tile_selfattention_pa_t_kernel(tc, X, Wq, bq, Wv, bv, out_0, out_1):
             score_rows = out_0[b].rearrange("(p m) j -> p m j", m=TOKEN_TILES)
             nc.sync.dma_start(out=score_rows[:, m0 : m0 + STORE_TILES, :], in_=score_sb[:])
 
-        x_grouped = transpose_x(0)
-        x_mx = new_mx("x")
-        quantise_tiles(x_grouped, x_mx, 0)
-        quantise_tiles(x_grouped, x_mx, QUANT_TILES)
-        q_mx = None
-        v_mx = None
-
-        for b in range(B):
-            v_sb = work.tile([P, TOKEN_TILES, D], F32)
-            v_grouped = work.tile([P, HALVES, D, PACK], BF16, align_bytes=64)
-            v_by_half = v_sb[:].rearrange("p (t h) d -> p h d t", h=HALVES)
-            for h in range(HALVES):
-                for t in range(PACK):
-                    value_bank(x_mx, v_sb, HALVES * t + h)
-                if b > 0:
-                    score_pair(b - 1, q_mx, v_mx, QUANT_TILES + STORE_TILES * h, False)
-                gpsimd_cols = slice(0, D) if h == 0 else slice(0, D // 2)
-                nc.gpsimd.tensor_scalar(
-                    out=v_grouped[:, h, gpsimd_cols], in0=v_by_half[:, h, gpsimd_cols],
-                    scalar1=1.0, scalar2=0.0, op0=MULT, op1=ADD,
-                )
-            nc.scalar.copy(out=v_grouped[:, 1, D // 2 : D], in_=v_by_half[:, 1, D // 2 : D])
+        def score_pair_half(b, q_mx, v_mx, m0, h, score_sb):
+            for i in range(STORE_TILES):
+                score_bank(q_mx, v_mx, m0 + i, h, score_sb[:, i, half_cols(h)], False)
+            score_rows = out_0[b].rearrange("(p m) j -> p m j", m=TOKEN_TILES)
             nc.sync.dma_start(
-                out=out_1[b].rearrange("(p m) d -> p m d", m=TOKEN_TILES), in_=v_sb[:]
+                out=score_rows[:, m0 : m0 + STORE_TILES, half_cols(h)],
+                in_=score_sb[:, :, half_cols(h)],
             )
 
-            q_grouped = work.tile([P, TOKEN_TILES, P, PACK], BF16, align_bytes=64)
+        x_grouped = new_grouped()
+        x_mx = new_mx("x")
+        for n in range(TOKEN_TILES // PAIR):
+            transpose_x(0, x_grouped, [n])
+        quantise(wv_grouped[:].rearrange("p c t -> p (c t)"), wv_codes[:], wv_scales[:])
+        for m0 in range(0, TOKEN_TILES, PAIR):
+            quantise_tiles(x_grouped, x_mx, m0, PAIR)
+        bv_acc = psum.tile([P, D], F32, tag="proj")
+        nc.tensor.matmul(out=bv_acc[:], lhsT=ones[:], rhs=bv_row[:], start=True, stop=True)
+        bv_bc = const.tile([P, D], F32)
+        nc.scalar.copy(out=bv_bc[:], in_=bv_acc[:])
+        nc.scalar.copy(
+            out=wq_grouped[:], in_=wq_raw[:].rearrange("p t (j i) -> p i j t", i=PACK)
+        )
+        v_sb = work.tile([P, TOKEN_TILES, D], F32, tag="v_sb")
+        v_grouped = work.tile([P, HALVES, D, PACK], BF16, align_bytes=64, tag="v_grouped")
+        q_grouped = work.tile([P, TOKEN_TILES, P, PACK], BF16, align_bytes=64, tag="q_grouped")
+        q_mx = new_mx("q")
+        v_mx = new_mx("v")
+        values(0, x_mx, v_sb, 0)
+        quantise(wq_grouped[:].rearrange("p i j t -> p (i j t)"), wq_codes[:], wq_scales[:])
+        regroup(v_sb, v_grouped, 0, D // 2)
+        next_grouped = new_grouped()
+        transpose_x(1, next_grouped, [0, 1])
+        values(0, x_mx, v_sb, 1)
+        regroup(v_sb, v_grouped, 1, D // 2)
+        transpose_x(1, next_grouped, [2, 3])
+        q_banks = [query_product(x_mx, m) for m in range(QUANT_TILES)]
+        for m in (0, 1):
+            add_query_bias(q_banks[m], q_grouped, m)
+        quantise_half(v_grouped, v_mx, 0)
+        quantise_tiles(q_grouped, q_mx, 0, PAIR)
+        for m in (2, 3):
+            add_query_bias(q_banks[m], q_grouped, m)
+        q_banks = [query_product(x_mx, m) for m in (4, 5)]
+        first_scores = score_pool.tile([P, STORE_TILES, HALVES * D], F32, tag="score_sb")
+        score_pair_half(0, q_mx, v_mx, 0, 0, first_scores)
+        quantise_half(v_grouped, v_mx, 1)
+        quantise_tiles(q_grouped, q_mx, PAIR, PAIR)
+        add_query_bias(q_banks[0], q_grouped, 4)
+        add_query_bias(q_banks[1], q_grouped, 5)
+        q_banks = [query_product(x_mx, m) for m in (6, 7)]
+        score_pair_half(0, q_mx, v_mx, 0, 1, first_scores)
+        add_query_bias(q_banks[0], q_grouped, 6)
+        add_query_bias(q_banks[1], q_grouped, 7)
+        x_grouped = next_grouped
+        x_mx = new_mx("x")
+        quantise_tiles(x_grouped, x_mx, 0, QUANT_TILES)
+        quantise_tiles(x_grouped, x_mx, QUANT_TILES, QUANT_TILES)
+        quantise_tiles(q_grouped, q_mx, QUANT_TILES, QUANT_TILES)
+        score_pair(0, q_mx, v_mx, STORE_TILES, False)
+
+        for b in range(1, B):
+            v_sb = work.tile([P, TOKEN_TILES, D], F32, tag="v_sb")
+            v_grouped = work.tile([P, HALVES, D, PACK], BF16, align_bytes=64, tag="v_grouped")
+            values(b, x_mx, v_sb, 0)
+            score_pair(b - 1, q_mx, v_mx, QUANT_TILES, False)
+            regroup(v_sb, v_grouped, 0, D)
+            values(b, x_mx, v_sb, 1)
+            score_pair(b - 1, q_mx, v_mx, QUANT_TILES + STORE_TILES, False)
+            regroup(v_sb, v_grouped, 1, D // 2)
+
+            q_grouped = work.tile([P, TOKEN_TILES, P, PACK], BF16, align_bytes=64, tag="q_grouped")
             q_mx = new_mx("q")
             v_mx = new_mx("v")
             for m in range(QUANT_TILES):
                 query_bank(x_mx, q_grouped, m)
             if b + 1 < B:
-                x_grouped = transpose_x(b + 1)
+                x_grouped = new_grouped()
+                transpose_x(b + 1, x_grouped, [0, 1, 2, 3])
             quantise_half(v_grouped, v_mx, 0)
-            quantise_tiles(q_grouped, q_mx, 0)
+            quantise_tiles(q_grouped, q_mx, 0, QUANT_TILES)
             quantise_half(v_grouped, v_mx, 1)
             for m in range(QUANT_TILES, TOKEN_TILES):
                 query_bank(x_mx, q_grouped, m)
             if b + 1 < B:
                 x_mx = new_mx("x")
-                quantise_tiles(x_grouped, x_mx, 0)
-                quantise_tiles(x_grouped, x_mx, QUANT_TILES)
-            quantise_tiles(q_grouped, q_mx, QUANT_TILES)
+                quantise_tiles(x_grouped, x_mx, 0, QUANT_TILES)
+                quantise_tiles(x_grouped, x_mx, QUANT_TILES, QUANT_TILES)
+            quantise_tiles(q_grouped, q_mx, QUANT_TILES, QUANT_TILES)
 
             score_pair(b, q_mx, v_mx, 0, False)
             score_pair(b, q_mx, v_mx, STORE_TILES, b == B - 1)

@@ -98,7 +98,7 @@ def tile_selfattention_pa_t_kernel(tc, X, Wq, bq, Wv, bv, out_0, out_1):
         nc.sync.dma_start(out=bv_row[0:1, :], in_=bv.rearrange("(o d) -> o d", o=1))
         wq_raw = load_weight(Wq, "wq_raw")
         nc.sync.dma_start(out=bq_sb[:], in_=bq.rearrange("(p t) -> p t", t=PACK))
-        x_tiles.extend(load_x(b, QUANT_TILES) for b in range(1, B))
+        x_tiles.extend(load_x(b, TOKEN_TILES) for b in range(1, B))
 
         ones = const.tile([P, P], BF16)
         nc.vector.memset(ones[:], 1.0)
@@ -162,10 +162,10 @@ def tile_selfattention_pa_t_kernel(tc, X, Wq, bq, Wv, bv, out_0, out_1):
         def values(b, x_mx, v_sb, h):
             for t in range(PACK):
                 value_bank(x_mx, v_sb, HALVES * t + h)
-            nc.sync.dma_start(
-                out=out_1[b].rearrange("(p t h) d -> p h t d", h=HALVES, t=PACK)[:, h],
-                in_=v_sb[:].rearrange("p (t h) d -> p h t d", h=HALVES)[:, h],
-            )
+
+        def store_values(b, v_sb, m0, count):
+            v_rows = out_1[b].rearrange("(p m) d -> p m d", m=TOKEN_TILES)
+            nc.sync.dma_start(out=v_rows[:, m0 : m0 + count], in_=v_sb[:, m0 : m0 + count])
 
         def regroup(v_sb, v_grouped, h, split):
             v_by_half = v_sb[:].rearrange("p (t h) d -> p h d t", h=HALVES)
@@ -228,6 +228,8 @@ def tile_selfattention_pa_t_kernel(tc, X, Wq, bq, Wv, bv, out_0, out_1):
         next_grouped = new_grouped()
         transpose_x(1, next_grouped, [0, 1])
         values(0, x_mx, v_sb, 1)
+        store_values(0, v_sb, 0, QUANT_TILES)
+        store_values(0, v_sb, QUANT_TILES, QUANT_TILES)
         regroup(v_sb, v_grouped, 1, D // 2)
         transpose_x(1, next_grouped, [2, 3])
         q_banks = [query_product(x_mx, m) for m in range(QUANT_TILES)]
@@ -263,6 +265,7 @@ def tile_selfattention_pa_t_kernel(tc, X, Wq, bq, Wv, bv, out_0, out_1):
             regroup(v_sb, v_grouped, 0, D)
             values(b, x_mx, v_sb, 1)
             score_pair(b - 1, q_mx, v_mx, QUANT_TILES + STORE_TILES, False)
+            store_values(b, v_sb, 0, TOKEN_TILES)
             regroup(v_sb, v_grouped, 1, D // 2)
 
             q_grouped = work.tile([P, TOKEN_TILES, P, PACK], BF16, align_bytes=64, tag="q_grouped")

@@ -94,8 +94,8 @@ def tile_selfattention_pa_t_kernel(tc, X, Wq, bq, Wv, bv, out_0, out_1):
         nc.vector.memset(bv_row[:], 0.0)
         bq_sb = const.tile([P, PACK], BF16)
         wv_raw = load_weight(Wv, "wv_raw")
-        x_tiles = [load_x(0, PAIR)]
         nc.sync.dma_start(out=bv_row[0:1, :], in_=bv.rearrange("(o d) -> o d", o=1))
+        x_tiles = [load_x(0, PAIR)]
         wq_raw = load_weight(Wq, "wq_raw")
         nc.sync.dma_start(out=bq_sb[:], in_=bq.rearrange("(p t) -> p t", t=PACK))
         x_tiles.extend(load_x(b, TOKEN_TILES) for b in range(1, B))
@@ -104,6 +104,11 @@ def tile_selfattention_pa_t_kernel(tc, X, Wq, bq, Wv, bv, out_0, out_1):
         nc.vector.memset(ones[:], 1.0)
         ident = const.tile([P, P], F32)
         make_identity(nc, ident[:])
+
+        bv_acc = psum.tile([P, D], F32, tag="proj")
+        nc.tensor.matmul(out=bv_acc[:], lhsT=ones[:], rhs=bv_row[:], start=True, stop=True)
+        bv_bc = const.tile([P, D], F32)
+        nc.scalar.copy(out=bv_bc[:], in_=bv_acc[:])
 
         wv_grouped = const.tile([P, D, PACK], BF16, align_bytes=64)
         nc.vector.tensor_copy(out=wv_grouped[:], in_=wv_raw[:].rearrange("p t c -> p c t"))
@@ -159,8 +164,10 @@ def tile_selfattention_pa_t_kernel(tc, X, Wq, bq, Wv, bv, out_0, out_1):
                 op=ADD,
             )
 
-        def values(b, x_mx, v_sb, h):
+        def values(x_mx, v_sb, h, beside=()):
             for t in range(PACK):
+                if beside:
+                    beside[t]()
                 value_bank(x_mx, v_sb, HALVES * t + h)
 
         def store_values(b, v_sb, m0, count):
@@ -194,6 +201,19 @@ def tile_selfattention_pa_t_kernel(tc, X, Wq, bq, Wv, bv, out_0, out_1):
             score_rows = out_0[b].rearrange("(p m) j -> p m j", m=TOKEN_TILES)
             nc.sync.dma_start(out=score_rows[:, m0 : m0 + STORE_TILES, :], in_=score_sb[:])
 
+        def score_steps(q_mx, v_mx, m0, score_sb):
+            return [
+                lambda i=i, h=h: score_bank(
+                    q_mx, v_mx, m0 + i, h, score_sb[:, i, half_cols(h)], False
+                )
+                for i in range(STORE_TILES)
+                for h in range(HALVES)
+            ]
+
+        def store_pair(b, m0, score_sb):
+            score_rows = out_0[b].rearrange("(p m) j -> p m j", m=TOKEN_TILES)
+            nc.sync.dma_start(out=score_rows[:, m0 : m0 + STORE_TILES, :], in_=score_sb[:])
+
         def score_pair_half(b, q_mx, v_mx, m0, h, score_sb):
             for i in range(STORE_TILES):
                 score_bank(q_mx, v_mx, m0 + i, h, score_sb[:, i, half_cols(h)], False)
@@ -210,10 +230,6 @@ def tile_selfattention_pa_t_kernel(tc, X, Wq, bq, Wv, bv, out_0, out_1):
         quantise(wv_grouped[:].rearrange("p c t -> p (c t)"), wv_codes[:], wv_scales[:])
         for m0 in range(0, TOKEN_TILES, PAIR):
             quantise_tiles(x_grouped, x_mx, m0, PAIR)
-        bv_acc = psum.tile([P, D], F32, tag="proj")
-        nc.tensor.matmul(out=bv_acc[:], lhsT=ones[:], rhs=bv_row[:], start=True, stop=True)
-        bv_bc = const.tile([P, D], F32)
-        nc.scalar.copy(out=bv_bc[:], in_=bv_acc[:])
         nc.scalar.copy(
             out=wq_grouped[:], in_=wq_raw[:].rearrange("p t (j i) -> p i j t", i=PACK)
         )
@@ -222,14 +238,14 @@ def tile_selfattention_pa_t_kernel(tc, X, Wq, bq, Wv, bv, out_0, out_1):
         q_grouped = work.tile([P, TOKEN_TILES, P, PACK], BF16, align_bytes=64, tag="q_grouped")
         q_mx = new_mx("q")
         v_mx = new_mx("v")
-        values(0, x_mx, v_sb, 0)
+        values(x_mx, v_sb, 0)
         quantise(wq_grouped[:].rearrange("p i j t -> p (i j t)"), wq_codes[:], wq_scales[:])
         regroup(v_sb, v_grouped, 0, D // 2)
         next_grouped = new_grouped()
-        transpose_x(1, next_grouped, [0, 1])
-        values(0, x_mx, v_sb, 1)
+        values(x_mx, v_sb, 1)
         store_values(0, v_sb, 0, QUANT_TILES)
         store_values(0, v_sb, QUANT_TILES, QUANT_TILES)
+        transpose_x(1, next_grouped, [0, 1])
         regroup(v_sb, v_grouped, 1, D // 2)
         transpose_x(1, next_grouped, [2, 3])
         q_banks = [query_product(x_mx, m) for m in range(QUANT_TILES)]
@@ -248,23 +264,26 @@ def tile_selfattention_pa_t_kernel(tc, X, Wq, bq, Wv, bv, out_0, out_1):
         add_query_bias(q_banks[1], q_grouped, 5)
         q_banks = [query_product(x_mx, m) for m in (6, 7)]
         score_pair_half(0, q_mx, v_mx, 0, 1, first_scores)
+        quantise_tiles(q_grouped, q_mx, QUANT_TILES, PAIR)
         add_query_bias(q_banks[0], q_grouped, 6)
         add_query_bias(q_banks[1], q_grouped, 7)
         x_grouped = next_grouped
         x_mx = new_mx("x")
         quantise_tiles(x_grouped, x_mx, 0, QUANT_TILES)
+        quantise_tiles(q_grouped, q_mx, QUANT_TILES + PAIR, PAIR)
         quantise_tiles(x_grouped, x_mx, QUANT_TILES, QUANT_TILES)
-        quantise_tiles(q_grouped, q_mx, QUANT_TILES, QUANT_TILES)
         score_pair(0, q_mx, v_mx, STORE_TILES, False)
 
         for b in range(1, B):
             v_sb = work.tile([P, TOKEN_TILES, D], F32, tag="v_sb")
             v_grouped = work.tile([P, HALVES, D, PACK], BF16, align_bytes=64, tag="v_grouped")
-            values(b, x_mx, v_sb, 0)
-            score_pair(b - 1, q_mx, v_mx, QUANT_TILES, False)
-            regroup(v_sb, v_grouped, 0, D)
-            values(b, x_mx, v_sb, 1)
-            score_pair(b - 1, q_mx, v_mx, QUANT_TILES + STORE_TILES, False)
+            for h in range(HALVES):
+                m0 = QUANT_TILES + STORE_TILES * h
+                score_sb = score_pool.tile([P, STORE_TILES, HALVES * D], F32, tag="score_sb")
+                values(x_mx, v_sb, h, score_steps(q_mx, v_mx, m0, score_sb))
+                store_pair(b - 1, m0, score_sb)
+                if h == 0:
+                    regroup(v_sb, v_grouped, 0, D)
             store_values(b, v_sb, 0, TOKEN_TILES)
             regroup(v_sb, v_grouped, 1, D // 2)
 
@@ -284,8 +303,9 @@ def tile_selfattention_pa_t_kernel(tc, X, Wq, bq, Wv, bv, out_0, out_1):
             if b + 1 < B:
                 x_mx = new_mx("x")
                 quantise_tiles(x_grouped, x_mx, 0, QUANT_TILES)
-                quantise_tiles(x_grouped, x_mx, QUANT_TILES, QUANT_TILES)
             quantise_tiles(q_grouped, q_mx, QUANT_TILES, QUANT_TILES)
+            if b + 1 < B:
+                quantise_tiles(x_grouped, x_mx, QUANT_TILES, QUANT_TILES)
 
             score_pair(b, q_mx, v_mx, 0, False)
             score_pair(b, q_mx, v_mx, STORE_TILES, b == B - 1)

@@ -111,7 +111,10 @@ def tile_selfattention_pa_t_kernel(tc, X, Wq, bq, Wv, bv, out_0, out_1):
         nc.scalar.copy(out=bv_bc[:], in_=bv_acc[:])
 
         wv_grouped = const.tile([P, D, PACK], BF16, align_bytes=64)
-        nc.vector.tensor_copy(out=wv_grouped[:], in_=wv_raw[:].rearrange("p t c -> p c t"))
+        nc.vector.tensor_copy(
+            out=wv_grouped[:].rearrange("p (j i) t -> p j t i", i=PACK),
+            in_=wv_raw[:].rearrange("p t (j i) -> p j t i", i=PACK),
+        )
         wq_grouped = const.tile([P, PACK, P, PACK], BF16, align_bytes=64)
         wv_codes = const.tile([P, D], U32, align_bytes=64)
         wv_scales = const.tile([P, D], U8, align_bytes=64)
@@ -164,11 +167,13 @@ def tile_selfattention_pa_t_kernel(tc, X, Wq, bq, Wv, bv, out_0, out_1):
                 op=ADD,
             )
 
-        def values(x_mx, v_sb, h, beside=()):
+        def values(x_mx, v_sb, h, beside=(), between=None):
             for t in range(PACK):
                 if beside:
                     beside[t]()
                 value_bank(x_mx, v_sb, HALVES * t + h)
+                if t == 2 and between:
+                    between()
 
         def store_values(b, v_sb, m0, count):
             v_rows = out_1[b].rearrange("(p m) d -> p m d", m=TOKEN_TILES)
@@ -231,7 +236,8 @@ def tile_selfattention_pa_t_kernel(tc, X, Wq, bq, Wv, bv, out_0, out_1):
         for m0 in range(0, TOKEN_TILES, PAIR):
             quantise_tiles(x_grouped, x_mx, m0, PAIR)
         nc.scalar.copy(
-            out=wq_grouped[:], in_=wq_raw[:].rearrange("p t (j i) -> p i j t", i=PACK)
+            out=wq_grouped[:].rearrange("p i j t -> p j t i"),
+            in_=wq_raw[:].rearrange("p t (j i) -> p j t i", i=PACK),
         )
         v_sb = work.tile([P, TOKEN_TILES, D], F32, tag="v_sb")
         v_grouped = work.tile([P, HALVES, D, PACK], BF16, align_bytes=64, tag="v_grouped")
@@ -239,14 +245,18 @@ def tile_selfattention_pa_t_kernel(tc, X, Wq, bq, Wv, bv, out_0, out_1):
         q_mx = new_mx("q")
         v_mx = new_mx("v")
         values(x_mx, v_sb, 0)
-        quantise(wq_grouped[:].rearrange("p i j t -> p (i j t)"), wq_codes[:], wq_scales[:])
         regroup(v_sb, v_grouped, 0, D // 2)
         next_grouped = new_grouped()
-        values(x_mx, v_sb, 1)
+        values(
+            x_mx, v_sb, 1,
+            between=lambda: quantise(
+                wq_grouped[:].rearrange("p i j t -> p (i j t)"), wq_codes[:], wq_scales[:]
+            ),
+        )
         store_values(0, v_sb, 0, QUANT_TILES)
         store_values(0, v_sb, QUANT_TILES, QUANT_TILES)
         transpose_x(1, next_grouped, [0, 1])
-        regroup(v_sb, v_grouped, 1, D // 2)
+        regroup(v_sb, v_grouped, 1, 3 * D // 8)
         transpose_x(1, next_grouped, [2, 3])
         q_banks = [query_product(x_mx, m) for m in range(QUANT_TILES)]
         for m in (0, 1):

@@ -105,6 +105,15 @@ def tile_selfattention_pa_t_kernel(tc, X, Wq, bq, Wv, bv, out_0, out_1):
         ident = const.tile([P, P], F32)
         make_identity(nc, ident[:])
 
+        warm = const.tile([P, D], BF16)
+        nc.vector.memset(warm[:], 1.0)
+
+        def keep_tensor_busy(count):
+            for n in range(count):
+                idle_acc = psum.tile([P, D], F32, tag="proj")
+                nc.tensor.matmul(out=idle_acc[:], lhsT=ones[:], rhs=warm[:], start=True, stop=True)
+
+        keep_tensor_busy(6)
         bv_acc = psum.tile([P, D], F32, tag="proj")
         nc.tensor.matmul(out=bv_acc[:], lhsT=ones[:], rhs=bv_row[:], start=True, stop=True)
         bv_bc = const.tile([P, D], F32)
@@ -232,6 +241,7 @@ def tile_selfattention_pa_t_kernel(tc, X, Wq, bq, Wv, bv, out_0, out_1):
         x_mx = new_mx("x")
         for n in range(TOKEN_TILES // PAIR):
             transpose_x(0, x_grouped, [n])
+            keep_tensor_busy(1)
         quantise(wv_grouped[:].rearrange("p c t -> p (c t)"), wv_codes[:], wv_scales[:])
         for m0 in range(0, TOKEN_TILES, PAIR):
             quantise_tiles(x_grouped, x_mx, m0, PAIR)

@@ -113,7 +113,7 @@ def tile_selfattention_pa_t_kernel(tc, X, Wq, bq, Wv, bv, out_0, out_1):
                 idle_acc = psum.tile([P, D], F32, tag="proj")
                 nc.tensor.matmul(out=idle_acc[:], lhsT=ones[:], rhs=warm[:], start=True, stop=True)
 
-        keep_tensor_busy(6)
+        keep_tensor_busy(4)
         bv_acc = psum.tile([P, D], F32, tag="proj")
         nc.tensor.matmul(out=bv_acc[:], lhsT=ones[:], rhs=bv_row[:], start=True, stop=True)
         bv_bc = const.tile([P, D], F32)
@@ -305,7 +305,7 @@ def tile_selfattention_pa_t_kernel(tc, X, Wq, bq, Wv, bv, out_0, out_1):
                 if h == 0:
                     regroup(v_sb, v_grouped, 0, D)
             store_values(b, v_sb, 0, TOKEN_TILES)
-            regroup(v_sb, v_grouped, 1, D // 2)
+            regroup(v_sb, v_grouped, 1, 3 * D // 8)
 
             q_grouped = work.tile([P, TOKEN_TILES, P, PACK], BF16, align_bytes=64, tag="q_grouped")
             q_mx = new_mx("q")

import math
from contextlib import ExitStack

import concourse.mybir as mybir
from concourse.masks import make_identity

BF16 = mybir.dt.bfloat16
F32 = mybir.dt.float32
U32 = mybir.dt.uint32
U8 = mybir.dt.uint8
FP8X4 = mybir.dt.float8_e4m3fn_x4
ADD = mybir.AluOpType.add
MULT = mybir.AluOpType.mult

B, S, D = 4, 1024, 512
P = 128
PACK = 4
TOKEN_TILES = S // P
HALVES = 2
QUANT_TILES = 4
PAIR = 2
STORE_TILES = 2
INV_SQRT_D = 1.0 / math.sqrt(D)

FLOPS = 2 * B * S * D * D * 2 + 2 * B * S * D * S


def tile_selfattention_pa_t_kernel(tc, X, Wq, bq, Wv, bv, out_0, out_1):
    nc = tc.nc
    with ExitStack() as stack:
        stack.enter_context(tc.manual_schedule())
        const = stack.enter_context(tc.tile_pool(name="const", bufs=1))
        x_pool = stack.enter_context(tc.tile_pool(name="x_in", bufs=B))
        work = stack.enter_context(tc.tile_pool(name="work", bufs=2))
        score_pool = stack.enter_context(tc.tile_pool(name="score_out", bufs=5))
        psum = stack.enter_context(tc.psum_pool(name="psum", bufs=4))

        def tile_cols(m, count=1):
            return slice(m * P, (m + count) * P)

        def half_cols(h):
            return slice(h * D, (h + 1) * D)

        def load_x(b, load_tiles):
            x_sb = x_pool.tile([P, TOKEN_TILES, D], BF16, tag="x")
            x_rows = X[b].rearrange("(p m) d -> p m d", m=TOKEN_TILES)
            for m0 in range(0, TOKEN_TILES, load_tiles):
                tiles = slice(m0, m0 + load_tiles)
                nc.sync.dma_start(out=x_sb[:, tiles, :], in_=x_rows[:, tiles, :])
            return x_sb

        def load_weight(w, name):
            raw = const.tile([P, PACK, D], BF16, name=name)
            nc.sync.dma_start(
                out=raw[:].rearrange("p (u e) c -> p u e c", u=2),
                in_=w.rearrange("(u p e) c -> p u e c", u=2, e=2),
            )
            return raw

        def quantise(grouped, codes, scales):
            nc.vector.quantize_mx(out=codes.bitcast(FP8X4), scales=scales, in_=grouped)

        def quantise_tiles(grouped, mx, m0, count):
            quantise(
                grouped[:, m0 : m0 + count].rearrange("p m k t -> p (m k t)"),
                mx[0][:, tile_cols(m0, count)],
                mx[1][:, tile_cols(m0, count)],
            )

        def quantise_half(v_grouped, mx, h):
            quantise(
                v_grouped[:, h].rearrange("p d t -> p (d t)"),
                mx[0][:, half_cols(h)],
                mx[1][:, half_cols(h)],
            )

        def new_mx(name):
            codes = work.tile([P, S], U32, align_bytes=64, name=name + "_codes")
            scales = work.tile([P, S], U8, align_bytes=64, name=name + "_scales")
            return codes, scales

        def mx_pass(acc, lhs, lhs_cols, rhs, rhs_cols):
            nc.tensor.matmul_mx(
                out=acc,
                lhsT=lhs[0][:, lhs_cols].bitcast(FP8X4),
                lhsT_scale=lhs[1][:, lhs_cols],
                rhs=rhs[0][:, rhs_cols].bitcast(FP8X4),
                rhs_scale=rhs[1][:, rhs_cols],
                start=True,
                stop=True,
            )

        bv_row = const.tile([P, D], BF16)
        nc.vector.memset(bv_row[:], 0.0)
        bq_sb = const.tile([P, PACK], BF16)
        wv_raw = load_weight(Wv, "wv_raw")
        nc.sync.dma_start(out=bv_row[0:1, :], in_=bv.rearrange("(o d) -> o d", o=1))
        x_tiles = [load_x(0, PAIR)]
        wq_raw = load_weight(Wq, "wq_raw")
        nc.sync.dma_start(out=bq_sb[:], in_=bq.rearrange("(p t) -> p t", t=PACK))
        x_tiles.extend(load_x(b, TOKEN_TILES) for b in range(1, B))

        ones = const.tile([P, P], BF16)
        nc.vector.memset(ones[:], 1.0)
        ident = const.tile([P, P], F32)
        make_identity(nc, ident[:])

        warm = const.tile([P, D], BF16)
        nc.vector.memset(warm[:], 1.0)

        def keep_tensor_busy(count):
            for n in range(count):
                idle_acc = psum.tile([P, D], F32, tag="proj")
                nc.tensor.matmul(out=idle_acc[:], lhsT=ones[:], rhs=warm[:], start=True, stop=True)

        keep_tensor_busy(4)
        bv_acc = psum.tile([P, D], F32, tag="proj")
        nc.tensor.matmul(out=bv_acc[:], lhsT=ones[:], rhs=bv_row[:], start=True, stop=True)
        bv_bc = const.tile([P, D], F32)
        nc.scalar.copy(out=bv_bc[:], in_=bv_acc[:])

        wv_grouped = const.tile([P, D, PACK], BF16, align_bytes=64)
        nc.vector.tensor_copy(
            out=wv_grouped[:].rearrange("p (j i) t -> p j t i", i=PACK),
            in_=wv_raw[:].rearrange("p t (j i) -> p j t i", i=PACK),
        )
        wq_grouped = const.tile([P, PACK, P, PACK], BF16, align_bytes=64)
        wv_codes = const.tile([P, D], U32, align_bytes=64)
        wv_scales = const.tile([P, D], U8, align_bytes=64)
        wq_codes = const.tile([P, D], U32, align_bytes=64)
        wq_scales = const.tile([P, D], U8, align_bytes=64)
        wv_mx = (wv_codes, wv_scales)
        wq_mx = (wq_codes, wq_scales)

        def transpose_x(b, x_grouped, bank_list):
            x_words = x_tiles[b][:].bitcast(F32)
            x_grouped_words = x_grouped[:].bitcast(F32)
            banks = []
            for n in bank_list:
                xt = psum.tile([P, 2, 2, P], F32, tag="side")
                for i in range(2):
                    for u in range(2):
                        nc.tensor.transpose(
                            xt[:, i, u, :], x_words[:, 2 * n + i, u * P : (u + 1) * P], ident[:]
                        )
                banks.append(xt)
            for n, xt in zip(bank_list, banks):
                nc.scalar.copy(
                    out=x_grouped_words[:, 2 * n : 2 * n + 2, :, :],
                    in_=xt[:].rearrange("p i u k -> p i k u"),
                )

        def new_grouped():
            x_grouped = work.tile([P, TOKEN_TILES, P, PACK], BF16, align_bytes=64)
            return x_grouped

        def value_bank(x_mx, v_sb, m):
            acc = psum.tile([P, D], F32, tag="proj")
            mx_pass(acc[:], x_mx, tile_cols(m), wv_mx, slice(0, D))
            nc.vector.tensor_tensor(out=v_sb[:, m, :], in0=acc[:], in1=bv_bc[:], op=ADD)

        def query_product(x_mx, m):
            acc = psum.tile([P, PACK, P], F32, tag="proj")
            for t in range(PACK):
                mx_pass(acc[:, t, :], wq_mx, tile_cols(t), x_mx, tile_cols(m))
            return acc

        def query_bank(x_mx, q_grouped, m):
            add_query_bias(query_product(x_mx, m), q_grouped, m)

        def add_query_bias(acc, q_grouped, m):
            nc.vector.tensor_tensor(
                out=q_grouped[:, m],
                in0=acc[:].rearrange("p t k -> p k t"),
                in1=bq_sb[:].unsqueeze(1).to_broadcast([P, P, PACK]),
                op=ADD,
            )

        def values(x_mx, v_sb, h, beside=(), between=None):
            for t in range(PACK):
                if beside:
                    beside[t]()
                value_bank(x_mx, v_sb, HALVES * t + h)
                if t == 2 and between:
                    between()

        def store_values(b, v_sb, m0, count):
            v_rows = out_1[b].rearrange("(p m) d -> p m d", m=TOKEN_TILES)
            nc.sync.dma_start(out=v_rows[:, m0 : m0 + count], in_=v_sb[:, m0 : m0 + count])

        def regroup(v_sb, v_grouped, h, split):
            v_by_half = v_sb[:].rearrange("p (t h) d -> p h d t", h=HALVES)
            nc.gpsimd.tensor_scalar(
                out=v_grouped[:, h, 0:split], in0=v_by_half[:, h, 0:split],
                scalar1=1.0, scalar2=0.0, op0=MULT, op1=ADD,
            )
            if split < D:
                nc.scalar.copy(out=v_grouped[:, h, split:D], in_=v_by_half[:, h, split:D])

        def score_bank(q_mx, v_mx, m, h, out_cols, on_vector):
            acc = psum.tile([P, D], F32, tag="side")
            mx_pass(acc[:], q_mx, tile_cols(m), v_mx, half_cols(h))
            if on_vector:
                nc.vector.tensor_scalar_mul(out=out_cols, in0=acc[:], scalar1=INV_SQRT_D)
            else:
                nc.scalar.mul(out=out_cols, in_=acc[:], mul=INV_SQRT_D)

        def score_pair(b, q_mx, v_mx, m0, vector_helps):
            score_sb = score_pool.tile([P, STORE_TILES, HALVES * D], F32, tag="score_sb")
            for i in range(STORE_TILES):
                for h in range(HALVES):
                    score_bank(
                        q_mx, v_mx, m0 + i, h, score_sb[:, i, half_cols(h)], vector_helps and h == 1
                    )
            score_rows = out_0[b].rearrange("(p m) j -> p m j", m=TOKEN_TILES)
            nc.sync.dma_start(out=score_rows[:, m0 : m0 + STORE_TILES, :], in_=score_sb[:])

        def score_steps(q_mx, v_mx, m0, score_sb):
            return [
                lambda i=i, h=h: score_bank(
                    q_mx, v_mx, m0 + i, h, score_sb[:, i, half_cols(h)], False
                )
                for i in range(STORE_TILES)
                for h in range(HALVES)
            ]

        def store_pair(b, m0, score_sb):
            score_rows = out_0[b].rearrange("(p m) j -> p m j", m=TOKEN_TILES)
            nc.sync.dma_start(out=score_rows[:, m0 : m0 + STORE_TILES, :], in_=score_sb[:])

        def score_pair_half(b, q_mx, v_mx, m0, h, score_sb):
            for i in range(STORE_TILES):
                score_bank(q_mx, v_mx, m0 + i, h, score_sb[:, i, half_cols(h)], False)
            score_rows = out_0[b].rearrange("(p m) j -> p m j", m=TOKEN_TILES)
            nc.sync.dma_start(
                out=score_rows[:, m0 : m0 + STORE_TILES, half_cols(h)],
                in_=score_sb[:, :, half_cols(h)],
            )

        x_grouped = new_grouped()
        x_mx = new_mx("x")
        for n in range(TOKEN_TILES // PAIR):
            transpose_x(0, x_grouped, [n])
            keep_tensor_busy(1)
        quantise(wv_grouped[:].rearrange("p c t -> p (c t)"), wv_codes[:], wv_scales[:])
        for m0 in range(0, TOKEN_TILES, PAIR):
            quantise_tiles(x_grouped, x_mx, m0, PAIR)
        nc.scalar.copy(
            out=wq_grouped[:].rearrange("p i j t -> p j t i"),
            in_=wq_raw[:].rearrange("p t (j i) -> p j t i", i=PACK),
        )
        v_sb = work.tile([P, TOKEN_TILES, D], F32, tag="v_sb")
        v_grouped = work.tile([P, HALVES, D, PACK], BF16, align_bytes=64, tag="v_grouped")
        q_grouped = work.tile([P, TOKEN_TILES, P, PACK], BF16, align_bytes=64, tag="q_grouped")
        q_mx = new_mx("q")
        v_mx = new_mx("v")
        values(x_mx, v_sb, 0)
        regroup(v_sb, v_grouped, 0, D // 2)
        next_grouped = new_grouped()
        values(
            x_mx, v_sb, 1,
            between=lambda: quantise(
                wq_grouped[:].rearrange("p i j t -> p (i j t)"), wq_codes[:], wq_scales[:]
            ),
        )
        store_values(0, v_sb, 0, QUANT_TILES)
        store_values(0, v_sb, QUANT_TILES, QUANT_TILES)
        transpose_x(1, next_grouped, [0, 1])
        regroup(v_sb, v_grouped, 1, 3 * D // 8)
        transpose_x(1, next_grouped, [2, 3])
        q_banks = [query_product(x_mx, m) for m in range(QUANT_TILES)]
        for m in (0, 1):
            add_query_bias(q_banks[m], q_grouped, m)
        quantise_half(v_grouped, v_mx, 0)
        quantise_tiles(q_grouped, q_mx, 0, PAIR)
        for m in (2, 3):
            add_query_bias(q_banks[m], q_grouped, m)
        q_banks = [query_product(x_mx, m) for m in (4, 5)]
        first_scores = score_pool.tile([P, STORE_TILES, HALVES * D], F32, tag="score_sb")
        score_pair_half(0, q_mx, v_mx, 0, 0, first_scores)
        quantise_half(v_grouped, v_mx, 1)
        quantise_tiles(q_grouped, q_mx, PAIR, PAIR)
        add_query_bias(q_banks[0], q_grouped, 4)
        add_query_bias(q_banks[1], q_grouped, 5)
        q_banks = [query_product(x_mx, m) for m in (6, 7)]
        score_pair_half(0, q_mx, v_mx, 0, 1, first_scores)
        quantise_tiles(q_grouped, q_mx, QUANT_TILES, PAIR)
        add_query_bias(q_banks[0], q_grouped, 6)
        add_query_bias(q_banks[1], q_grouped, 7)
        x_grouped = next_grouped
        x_mx = new_mx("x")
        quantise_tiles(x_grouped, x_mx, 0, QUANT_TILES)
        quantise_tiles(q_grouped, q_mx, QUANT_TILES + PAIR, PAIR)
        quantise_tiles(x_grouped, x_mx, QUANT_TILES, QUANT_TILES)
        score_pair(0, q_mx, v_mx, STORE_TILES, False)

        for b in range(1, B):
            v_sb = work.tile([P, TOKEN_TILES, D], F32, tag="v_sb")
            v_grouped = work.tile([P, HALVES, D, PACK], BF16, align_bytes=64, tag="v_grouped")
            for h in range(HALVES):
                m0 = QUANT_TILES + STORE_TILES * h
                score_sb = score_pool.tile([P, STORE_TILES, HALVES * D], F32, tag="score_sb")
                values(x_mx, v_sb, h, score_steps(q_mx, v_mx, m0, score_sb))
                store_pair(b - 1, m0, score_sb)
                if h == 0:
                    regroup(v_sb, v_grouped, 0, D)
            store_values(b, v_sb, 0, TOKEN_TILES)
            regroup(v_sb, v_grouped, 1, 3 * D // 8)

            q_grouped = work.tile([P, TOKEN_TILES, P, PACK], BF16, align_bytes=64, tag="q_grouped")
            q_mx = new_mx("q")
            v_mx = new_mx("v")
            for m in range(QUANT_TILES):
                query_bank(x_mx, q_grouped, m)
            if b + 1 < B:
                x_grouped = new_grouped()
                transpose_x(b + 1, x_grouped, [0, 1, 2, 3])
            quantise_half(v_grouped, v_mx, 0)
            quantise_tiles(q_grouped, q_mx, 0, QUANT_TILES)
            quantise_half(v_grouped, v_mx, 1)
            for m in range(QUANT_TILES, TOKEN_TILES):
                query_bank(x_mx, q_grouped, m)
            if b + 1 < B:
                x_mx = new_mx("x")
                quantise_tiles(x_grouped, x_mx, 0, QUANT_TILES)
            quantise_tiles(q_grouped, q_mx, QUANT_TILES, QUANT_TILES)
            if b + 1 < B:
                quantise_tiles(x_grouped, x_mx, QUANT_TILES, QUANT_TILES)

            score_pair(b, q_mx, v_mx, 0, False)
            score_pair(b, q_mx, v_mx, STORE_TILES, b == B - 1)

        for m0 in range(QUANT_TILES, TOKEN_TILES, STORE_TILES):
            score_pair(B - 1, q_mx, v_mx, m0, True)
